import numpy as np
import ml_dtypes


def mxq(x, axis, fmt="e4m3"):
    dtype, down = {"e4m3": (ml_dtypes.float8_e4m3fn, 7), "e5m2": (ml_dtypes.float8_e5m2, 14)}[fmt]
    v = np.moveaxis(np.asarray(x, np.float32).astype(ml_dtypes.bfloat16).astype(np.float64), axis, -1)
    blocks = v.reshape(v.shape[:-1] + (-1, 32))
    amax = np.abs(blocks).max(-1, keepdims=True)
    byte = np.maximum(np.where(amax > 0, np.frexp(amax)[1] - 1 + 127, 0) - down, 1)
    scale = np.exp2(byte - 127.0)
    codes = (blocks / scale).astype(np.float32).astype(dtype).astype(np.float64)
    return np.moveaxis((codes * scale).reshape(v.shape), -1, axis)


WIDE = False


def mx_kscale(k):
    if not WIDE:
        return np.ones(k)
    levels = np.array([20, -20, 10, -10, 0])
    a = np.random.permutation(np.resize(levels, k // 512 * 4)).reshape(k // 512, 4)
    idx = np.arange(k)
    return np.exp2(a[idx // 512, idx % 128 // 32])


BF16 = ml_dtypes.bfloat16


def bf(x):
    return np.asarray(x, np.float32).astype(BF16)


def f64(x):
    return np.asarray(x).astype(np.float64)


B, IN, OUT, R, Q, ORD = 16384, 1024, 1024, 8, 512, 3
K = R ** ORD


def kron_of(Z):
    kron = Z[0]
    for j in range(1, ORD):
        kron = kron[None] * Z[j].reshape((R,) + (1,) * j + (B,))
    return kron.reshape((-1, B))


def setup_inputs():
    s = mx_kscale(B)
    z = np.random.standard_normal((ORD, R, B))
    z[ORD - 1] *= s[None, :]
    g = np.random.standard_normal((Q, K)) / np.sqrt(K)
    go = np.random.standard_normal((Q, B)) * np.exp2(np.random.randint(-12, 1, (1, B))) * 0.25 / s[None, :]
    return {"z": bf(z), "G2": bf(g), "grad_out": bf(go)}


def reference(z, G2, grad_out):
    kron = kron_of(f64(z))
    return mxq(f64(grad_out), 1, "e5m2") @ mxq(kron, 1, "e4m3").T

@@ -1,0 +1,164 @@
+from contextlib import ExitStack
+
+import concourse.mybir as mybir
+from concourse.masks import make_identity
+
+F32 = mybir.dt.float32
+BF16 = mybir.dt.bfloat16
+U32 = mybir.dt.uint32
+U8 = mybir.dt.uint8
+E4M3_X4 = mybir.dt.float8_e4m3fn_x4
+E5M2_X4 = mybir.dt.float8_e5m2_x4
+MULT = mybir.AluOpType.mult
+
+P = 128
+PACK = 4
+PAIR = 2
+PASS = P * PACK
+RANK = 8
+Q = 512
+K = RANK * RANK * RANK
+SAMPLES = 16384
+N_PASSES = SAMPLES // PASS
+Q_TILES = Q // P
+BANK = 512
+CHUNK_PASSES = 2
+LOOKAHEAD = 2
+
+FLOPS = 2 * Q * K * SAMPLES
+BYTES = 3 * RANK * SAMPLES * 2 + Q * SAMPLES * 2 + Q * K * 4
+
+
+def tile_fast_tucker_taylor_pa_t_kernel(tc, z, G2, grad_out, out):
+    nc = tc.nc
+    with ExitStack() as ctx:
+        keep = ctx.enter_context(tc.tile_pool(name="keep", bufs=1))
+        loads = ctx.enter_context(tc.tile_pool(name="loads", bufs=6))
+        stage = ctx.enter_context(tc.tile_pool(name="stage", bufs=3))
+        results = ctx.enter_context(tc.tile_pool(name="results", bufs=Q_TILES))
+        psum_sums = ctx.enter_context(tc.psum_pool(name="psum_sums", bufs=1))
+        psum_z2 = ctx.enter_context(tc.psum_pool(name="psum_z2", bufs=1))
+        psum_turn = ctx.enter_context(tc.psum_pool(name="psum_turn", bufs=3))
+        ctx.enter_context(tc.manual_schedule())
+
+        n_slabs = 3 * RANK * SAMPLES // (PAIR * P * P)
+        z_runs = z.rearrange("j r (s w) -> (j r s) w", w=PAIR * P)
+        z_raw = keep.tile([P, n_slabs, PAIR * P], BF16)
+        nc.sync.dma_start(out=z_raw[:], in_=z_runs.rearrange("(m i) w -> i m w", i=P))
+
+        chunk_samples = CHUNK_PASSES * PASS
+        go_rows = grad_out.rearrange("(qt i) n -> i qt n", i=P)
+        go_chunks = []
+        for c in range(N_PASSES // CHUNK_PASSES):
+            go_sb = loads.tile([P, Q_TILES, chunk_samples], BF16)
+            nc.sync.dma_start(
+                out=go_sb[:], in_=go_rows[:, :, c * chunk_samples : (c + 1) * chunk_samples]
+            )
+            go_chunks.append(go_sb)
+
+        identity = keep.tile([P, P], F32)
+        make_identity(nc, identity[:])
+
+        slabs_per_factor = n_slabs // 3
+        z_banks = []
+        for j in range(3):
+            pool = psum_z2 if j == 2 else psum_turn
+            z_bank = pool.tile([P, BANK], F32, tag="z2" if j == 2 else "turned", name="z_bank%d" % j)
+            for i in range(slabs_per_factor):
+                nc.tensor.transpose(
+                    z_bank[:, i * P : (i + 1) * P],
+                    z_raw[:, j * slabs_per_factor + i, :].bitcast(F32),
+                    identity[:],
+                )
+            z_banks.append(z_bank)
+
+        z_by_pass = []
+        for j in range(2):
+            z_sb = keep.tile([P, N_PASSES, RANK, PACK], BF16, name="z_sb%d" % j)
+            nc.scalar.copy(
+                out=z_sb[:].bitcast(F32),
+                in_=z_banks[j][:].rearrange("p (r g u) -> p g r u", r=RANK, u=PAIR),
+            )
+            z_by_pass.append(z_sb)
+        z2_by_row = z_banks[2][:].bitcast(BF16).rearrange("p (c g t) -> p c g t", c=RANK, t=PACK)
+
+        z01 = keep.tile([P, N_PASSES, RANK * RANK, PACK], F32)
+        for b in range(RANK):
+            nc.vector.tensor_tensor(
+                out=z01[:, :, b * RANK : (b + 1) * RANK, :],
+                in0=z_by_pass[0][:],
+                in1=z_by_pass[1][:, :, b : b + 1, :].to_broadcast([P, N_PASSES, RANK, PACK]),
+                op=MULT,
+            )
+
+        sums = [psum_sums.tile([P, K], F32, name="sums%d" % qt) for qt in range(Q_TILES)]
+
+        def turn_grad_out(g):
+            go_words = go_chunks[g // CHUNK_PASSES][:].bitcast(F32)
+            first_word = (g % CHUNK_PASSES) * PASS // PAIR
+            grouped = stage.tile([P, Q * PACK], BF16, align_bytes=64)
+            grouped_words = grouped[:].bitcast(F32).rearrange("p (q u) -> p q u", u=PAIR)
+            rows_per_bank = BANK // PAIR
+            for h in range(Q // rows_per_bank):
+                turned = psum_turn.tile([P, PAIR, rows_per_bank], F32, tag="turned")
+                for u in range(PAIR):
+                    for i in range(rows_per_bank // P):
+                        nc.tensor.transpose(
+                            turned[:, u, i * P : (i + 1) * P],
+                            go_words[
+                                :,
+                                h * (rows_per_bank // P) + i,
+                                first_word + u * P : first_word + (u + 1) * P,
+                            ],
+                            identity[:],
+                        )
+                nc.scalar.copy(
+                    out=grouped_words[:, h * rows_per_bank : (h + 1) * rows_per_bank, :],
+                    in_=turned[:].rearrange("p u q -> p q u"),
+                )
+            return grouped
+
+        grouped_ahead = [turn_grad_out(g) for g in range(LOOKAHEAD)]
+
+        for g in range(N_PASSES):
+            kron_bf = stage.tile([P, K * PACK], BF16, align_bytes=64)
+            nc.vector.tensor_tensor(
+                out=kron_bf[:].rearrange("p (c x t) -> p c x t", c=RANK, t=PACK),
+                in0=z01[:, g : g + 1, :, :].to_broadcast([P, RANK, RANK * RANK, PACK]),
+                in1=z2_by_row[:, :, g : g + 1, :].to_broadcast([P, RANK, RANK * RANK, PACK]),
+                op=MULT,
+            )
+
+            go_codes = stage.tile([P, Q], U32, align_bytes=64)
+            go_scales = stage.tile([P, Q], U8, align_bytes=64)
+            nc.vector.quantize_mx(
+                out=go_codes[:].bitcast(E5M2_X4), scales=go_scales[:], in_=grouped_ahead[g][:]
+            )
+            kron_codes = stage.tile([P, K], U32, align_bytes=64)
+            kron_scales = stage.tile([P, K], U8, align_bytes=64)
+            nc.vector.quantize_mx(
+                out=kron_codes[:].bitcast(E4M3_X4), scales=kron_scales[:], in_=kron_bf[:]
+            )
+
+            for qt in range(Q_TILES):
+                q_cols = slice(qt * P, (qt + 1) * P)
+                nc.tensor.matmul_mx(
+                    out=sums[qt][:],
+                    lhsT=go_codes[:, q_cols].bitcast(E5M2_X4),
+                    lhsT_scale=go_scales[:, q_cols],
+                    rhs=kron_codes[:].bitcast(E4M3_X4),
+                    rhs_scale=kron_scales[:],
+                    start=(g == 0),
+                    stop=(g == N_PASSES - 1),
+                )
+
+            if g + LOOKAHEAD < N_PASSES:
+                grouped_ahead.append(turn_grad_out(g + LOOKAHEAD))
+
+        for qt in range(Q_TILES):
+            result = results.tile([P, K], F32)
+            if qt % 2 == 0:
+                nc.scalar.copy(out=result[:], in_=sums[qt][:])
+            else:
+                nc.vector.tensor_copy(out=result[:], in_=sums[qt][:])
+            nc.sync.dma_start(out=out[qt * P : (qt + 1) * P, :], in_=result[:])

@@ -23,7 +23,7 @@ N_PASSES = SAMPLES // PASS
 Q_TILES = Q // P
 BANK = 512
 CHUNK_PASSES = 2
-LOOKAHEAD = 2
+ROUND = 3
 
 FLOPS = 2 * Q * K * SAMPLES
 BYTES = 3 * RANK * SAMPLES * 2 + Q * SAMPLES * 2 + Q * K * 4
@@ -34,7 +34,9 @@ def tile_fast_tucker_taylor_pa_t_kernel(tc, z, G2, grad_out, out):
     with ExitStack() as ctx:
         keep = ctx.enter_context(tc.tile_pool(name="keep", bufs=1))
         loads = ctx.enter_context(tc.tile_pool(name="loads", bufs=6))
-        stage = ctx.enter_context(tc.tile_pool(name="stage", bufs=3))
+        stage = ctx.enter_context(tc.tile_pool(name="stage", bufs=2 * ROUND))
+        vector_kron = ctx.enter_context(tc.tile_pool(name="vector_kron", bufs=ROUND))
+        gpsimd_kron = ctx.enter_context(tc.tile_pool(name="gpsimd_kron", bufs=1))
         results = ctx.enter_context(tc.tile_pool(name="results", bufs=Q_TILES))
         psum_sums = ctx.enter_context(tc.psum_pool(name="psum_sums", bufs=1))
         psum_z2 = ctx.enter_context(tc.psum_pool(name="psum_z2", bufs=1))
@@ -80,7 +82,12 @@ def tile_fast_tucker_taylor_pa_t_kernel(tc, z, G2, grad_out, out):
                 in_=z_banks[j][:].rearrange("p (r g u) -> p g r u", r=RANK, u=PAIR),
             )
             z_by_pass.append(z_sb)
-        z2_by_row = z_banks[2][:].bitcast(BF16).rearrange("p (c g t) -> p c g t", c=RANK, t=PACK)
+        z2_sb = keep.tile([P, RANK, N_PASSES, PACK], BF16)
+        nc.scalar.copy(
+            out=z2_sb[:].bitcast(F32),
+            in_=z_banks[2][:].rearrange("p (c g u) -> p c g u", c=RANK, u=PAIR),
+        )
+        z2_psum = z_banks[2][:].bitcast(BF16).rearrange("p (c g t) -> p c g t", c=RANK, t=PACK)
 
         z01 = keep.tile([P, N_PASSES, RANK * RANK, PACK], F32)
         for b in range(RANK):
@@ -118,42 +125,53 @@ def tile_fast_tucker_taylor_pa_t_kernel(tc, z, G2, grad_out, out):
                 )
             return grouped
 
-        grouped_ahead = [turn_grad_out(g) for g in range(LOOKAHEAD)]
-
-        for g in range(N_PASSES):
-            kron_bf = stage.tile([P, K * PACK], BF16, align_bytes=64)
-            nc.vector.tensor_tensor(
+        def kron_of_pass(g):
+            if g % ROUND == ROUND - 1:
+                engine, pool, z2_rows = nc.gpsimd, gpsimd_kron, z2_sb
+            else:
+                engine, pool, z2_rows = nc.vector, vector_kron, z2_psum
+            kron_bf = pool.tile([P, K * PACK], BF16, align_bytes=64)
+            engine.tensor_tensor(
                 out=kron_bf[:].rearrange("p (c x t) -> p c x t", c=RANK, t=PACK),
                 in0=z01[:, g : g + 1, :, :].to_broadcast([P, RANK, RANK * RANK, PACK]),
-                in1=z2_by_row[:, :, g : g + 1, :].to_broadcast([P, RANK, RANK * RANK, PACK]),
+                in1=z2_rows[:, :, g : g + 1, :].to_broadcast([P, RANK, RANK * RANK, PACK]),
                 op=MULT,
             )
+            return kron_bf
 
-            go_codes = stage.tile([P, Q], U32, align_bytes=64)
-            go_scales = stage.tile([P, Q], U8, align_bytes=64)
-            nc.vector.quantize_mx(
-                out=go_codes[:].bitcast(E5M2_X4), scales=go_scales[:], in_=grouped_ahead[g][:]
-            )
-            kron_codes = stage.tile([P, K], U32, align_bytes=64)
-            kron_scales = stage.tile([P, K], U8, align_bytes=64)
-            nc.vector.quantize_mx(
-                out=kron_codes[:].bitcast(E4M3_X4), scales=kron_scales[:], in_=kron_bf[:]
-            )
+        def quantise(values, x4_dtype, operand):
+            n_rows = values.shape[1] // PACK
+            codes_name, scales_name = "%s_codes" % operand, "%s_scales" % operand
+            codes = stage.tile([P, n_rows], U32, align_bytes=64, name=codes_name, tag=codes_name)
+            scales = stage.tile([P, n_rows], U8, align_bytes=64, name=scales_name, tag=scales_name)
+            nc.vector.quantize_mx(out=codes[:].bitcast(x4_dtype), scales=scales[:], in_=values[:])
+            return codes, scales
 
-            for qt in range(Q_TILES):
-                q_cols = slice(qt * P, (qt + 1) * P)
-                nc.tensor.matmul_mx(
-                    out=sums[qt][:],
-                    lhsT=go_codes[:, q_cols].bitcast(E5M2_X4),
-                    lhsT_scale=go_scales[:, q_cols],
-                    rhs=kron_codes[:].bitcast(E4M3_X4),
-                    rhs_scale=kron_scales[:],
-                    start=(g == 0),
-                    stop=(g == N_PASSES - 1),
-                )
+        rounds = [range(first, min(first + ROUND, N_PASSES)) for first in range(0, N_PASSES, ROUND)]
+        go_next = [turn_grad_out(g) for g in rounds[0]]
 
-            if g + LOOKAHEAD < N_PASSES:
-                grouped_ahead.append(turn_grad_out(g + LOOKAHEAD))
+        for r in range(len(rounds)):
+            go_now = go_next
+            kron_now = [kron_of_pass(g) for g in rounds[r]]
+
+            if r + 1 < len(rounds):
+                go_next = [turn_grad_out(g) for g in rounds[r + 1]]
+
+            for g, go_bf, kron_bf in zip(rounds[r], go_now, kron_now):
+                go_codes, go_scales = quantise(go_bf, E5M2_X4, "go")
+                kron_codes, kron_scales = quantise(kron_bf, E4M3_X4, "kron")
+
+                for qt in range(Q_TILES):
+                    q_cols = slice(qt * P, (qt + 1) * P)
+                    nc.tensor.matmul_mx(
+                        out=sums[qt][:],
+                        lhsT=go_codes[:, q_cols].bitcast(E5M2_X4),
+                        lhsT_scale=go_scales[:, q_cols],
+                        rhs=kron_codes[:].bitcast(E4M3_X4),
+                        rhs_scale=kron_scales[:],
+                        start=(g == 0),
+                        stop=(g == N_PASSES - 1),
+                    )
 
         for qt in range(Q_TILES):
             result = results.tile([P, K], F32)

@@ -10,20 +10,22 @@ U8 = mybir.dt.uint8
 E4M3_X4 = mybir.dt.float8_e4m3fn_x4
 E5M2_X4 = mybir.dt.float8_e5m2_x4
 MULT = mybir.AluOpType.mult
+COPY = mybir.ActivationFunctionType.Copy
 
 P = 128
 PACK = 4
 PAIR = 2
 PASS = P * PACK
 RANK = 8
+RANK2 = RANK * RANK
 Q = 512
-K = RANK * RANK * RANK
+K = RANK * RANK2
 SAMPLES = 16384
 N_PASSES = SAMPLES // PASS
 Q_TILES = Q // P
 BANK = 512
 CHUNK_PASSES = 2
-ROUND = 3
+ROUND = 4
 
 FLOPS = 2 * Q * K * SAMPLES
 BYTES = 3 * RANK * SAMPLES * 2 + Q * SAMPLES * 2 + Q * K * 4
@@ -34,9 +36,11 @@ def tile_fast_tucker_taylor_pa_t_kernel(tc, z, G2, grad_out, out):
     with ExitStack() as ctx:
         keep = ctx.enter_context(tc.tile_pool(name="keep", bufs=1))
         loads = ctx.enter_context(tc.tile_pool(name="loads", bufs=6))
-        stage = ctx.enter_context(tc.tile_pool(name="stage", bufs=2 * ROUND))
-        vector_kron = ctx.enter_context(tc.tile_pool(name="vector_kron", bufs=ROUND))
+        turned_go = ctx.enter_context(tc.tile_pool(name="turned_go", bufs=2 * ROUND))
+        vector_kron = ctx.enter_context(tc.tile_pool(name="vector_kron", bufs=2))
         gpsimd_kron = ctx.enter_context(tc.tile_pool(name="gpsimd_kron", bufs=1))
+        scalar_kron = ctx.enter_context(tc.tile_pool(name="scalar_kron", bufs=2))
+        quantised = ctx.enter_context(tc.tile_pool(name="quantised", bufs=ROUND + 2))
         results = ctx.enter_context(tc.tile_pool(name="results", bufs=Q_TILES))
         psum_sums = ctx.enter_context(tc.psum_pool(name="psum_sums", bufs=1))
         psum_z2 = ctx.enter_context(tc.psum_pool(name="psum_z2", bufs=1))
@@ -82,14 +86,11 @@ def tile_fast_tucker_taylor_pa_t_kernel(tc, z, G2, grad_out, out):
                 in_=z_banks[j][:].rearrange("p (r g u) -> p g r u", r=RANK, u=PAIR),
             )
             z_by_pass.append(z_sb)
-        z2_sb = keep.tile([P, RANK, N_PASSES, PACK], BF16)
-        nc.scalar.copy(
-            out=z2_sb[:].bitcast(F32),
-            in_=z_banks[2][:].rearrange("p (c g u) -> p c g u", c=RANK, u=PAIR),
-        )
         z2_psum = z_banks[2][:].bitcast(BF16).rearrange("p (c g t) -> p c g t", c=RANK, t=PACK)
+        z2_f32 = keep.tile([P, RANK, N_PASSES, PACK], F32)
+        nc.scalar.copy(out=z2_f32[:], in_=z2_psum)
 
-        z01 = keep.tile([P, N_PASSES, RANK * RANK, PACK], F32)
+        z01 = keep.tile([P, N_PASSES, RANK2, PACK], F32)
         for b in range(RANK):
             nc.vector.tensor_tensor(
                 out=z01[:, :, b * RANK : (b + 1) * RANK, :],
@@ -103,7 +104,7 @@ def tile_fast_tucker_taylor_pa_t_kernel(tc, z, G2, grad_out, out):
         def turn_grad_out(g):
             go_words = go_chunks[g // CHUNK_PASSES][:].bitcast(F32)
             first_word = (g % CHUNK_PASSES) * PASS // PAIR
-            grouped = stage.tile([P, Q * PACK], BF16, align_bytes=64)
+            grouped = turned_go.tile([P, Q * PACK], BF16, align_bytes=64)
             grouped_words = grouped[:].bitcast(F32).rearrange("p (q u) -> p q u", u=PAIR)
             rows_per_bank = BANK // PAIR
             for h in range(Q // rows_per_bank):
@@ -125,41 +126,77 @@ def tile_fast_tucker_taylor_pa_t_kernel(tc, z, G2, grad_out, out):
                 )
             return grouped
 
-        def kron_of_pass(g):
-            if g % ROUND == ROUND - 1:
-                engine, pool, z2_rows = nc.gpsimd, gpsimd_kron, z2_sb
-            else:
-                engine, pool, z2_rows = nc.vector, vector_kron, z2_psum
-            kron_bf = pool.tile([P, K * PACK], BF16, align_bytes=64)
+        def kron_as_tensors(engine, pool, z2_rows, g, cs):
+            part = pool.tile([P, len(cs) * RANK2 * PACK], BF16, align_bytes=64, tag="c%d" % len(cs))
+            shape = [P, len(cs), RANK2, PACK]
             engine.tensor_tensor(
-                out=kron_bf[:].rearrange("p (c x t) -> p c x t", c=RANK, t=PACK),
-                in0=z01[:, g : g + 1, :, :].to_broadcast([P, RANK, RANK * RANK, PACK]),
-                in1=z2_rows[:, :, g : g + 1, :].to_broadcast([P, RANK, RANK * RANK, PACK]),
+                out=part[:].rearrange("p (c x t) -> p c x t", x=RANK2, t=PACK),
+                in0=z01[:, g : g + 1, :, :].to_broadcast(shape),
+                in1=z2_rows[:, cs[0] : cs[0] + len(cs), g : g + 1, :].to_broadcast(shape),
                 op=MULT,
             )
-            return kron_bf
+            return part
 
-        def quantise(values, x4_dtype, operand):
-            n_rows = values.shape[1] // PACK
+        def kron_on_vector(g, cs):
+            return kron_as_tensors(nc.vector, vector_kron, z2_psum, g, cs)
+
+        def kron_on_gpsimd(g, cs):
+            return kron_as_tensors(nc.gpsimd, gpsimd_kron, z2_f32, g, cs)
+
+        def kron_on_scalar(g, cs):
+            part = scalar_kron.tile([P, len(cs) * RANK2 * PACK], BF16, align_bytes=64)
+            part_rows = part[:].rearrange("p (c x t) -> p c x t", x=RANK2, t=PACK)
+            for i in range(len(cs)):
+                for t in range(PACK):
+                    nc.scalar.activation(
+                        out=part_rows[:, i, :, t],
+                        in_=z01[:, g, :, t],
+                        func=COPY,
+                        scale=z2_f32[:, cs[i], g, t : t + 1],
+                    )
+            return part
+
+        def quantise(parts, x4_dtype, operand):
             codes_name, scales_name = "%s_codes" % operand, "%s_scales" % operand
-            codes = stage.tile([P, n_rows], U32, align_bytes=64, name=codes_name, tag=codes_name)
-            scales = stage.tile([P, n_rows], U8, align_bytes=64, name=scales_name, tag=scales_name)
-            nc.vector.quantize_mx(out=codes[:].bitcast(x4_dtype), scales=scales[:], in_=values[:])
+            codes = quantised.tile([P, BANK], U32, align_bytes=64, name=codes_name, tag=codes_name)
+            scales = quantised.tile([P, BANK], U8, align_bytes=64, name=scales_name, tag=scales_name)
+            first_row = 0
+            for part in parts:
+                n_rows = part.shape[1] // PACK
+                rows = slice(first_row, first_row + n_rows)
+                nc.vector.quantize_mx(
+                    out=codes[:, rows].bitcast(x4_dtype), scales=scales[:, rows], in_=part[:]
+                )
+                first_row += n_rows
             return codes, scales
 
-        rounds = [range(first, min(first + ROUND, N_PASSES)) for first in range(0, N_PASSES, ROUND)]
-        go_next = [turn_grad_out(g) for g in rounds[0]]
+        all_c = range(RANK)
+        low_c = range(RANK // 2)
+        high_c = range(RANK // 2, RANK)
+        shared = ROUND - 2
+        n_rounds = N_PASSES // ROUND
 
-        for r in range(len(rounds)):
-            go_now = go_next
-            kron_now = [kron_of_pass(g) for g in rounds[r]]
+        go_next = [turn_grad_out(g) for g in range(ROUND)]
+        scalar_next = kron_on_scalar(shared, high_c)
 
-            if r + 1 < len(rounds):
-                go_next = [turn_grad_out(g) for g in rounds[r + 1]]
+        for r in range(n_rounds):
+            first = r * ROUND
+            go_now, scalar_now = go_next, scalar_next
+            kron_now = [
+                [kron_on_vector(first, all_c)],
+                [kron_on_vector(first + 1, all_c)],
+                [kron_on_vector(first + shared, low_c), scalar_now],
+                [kron_on_gpsimd(first + ROUND - 1, all_c)],
+            ]
 
-            for g, go_bf, kron_bf in zip(rounds[r], go_now, kron_now):
-                go_codes, go_scales = quantise(go_bf, E5M2_X4, "go")
-                kron_codes, kron_scales = quantise(kron_bf, E4M3_X4, "kron")
+            if r + 1 < n_rounds:
+                go_next = [turn_grad_out(first + ROUND + i) for i in range(ROUND)]
+                scalar_next = kron_on_scalar(first + ROUND + shared, high_c)
+
+            for i in range(ROUND):
+                g = first + i
+                go_codes, go_scales = quantise([go_now[i]], E5M2_X4, "go")
+                kron_codes, kron_scales = quantise(kron_now[i], E4M3_X4, "kron")
 
                 for qt in range(Q_TILES):
                     q_cols = slice(qt * P, (qt + 1) * P)

@@ -26,6 +26,9 @@ Q_TILES = Q // P
 BANK = 512
 CHUNK_PASSES = 2
 ROUND = 4
+SHARED = ROUND - 2
+SCALAR_ROWS = 6
+GPSIMD_ROWS = 2
 
 FLOPS = 2 * Q * K * SAMPLES
 BYTES = 3 * RANK * SAMPLES * 2 + Q * SAMPLES * 2 + Q * K * 4
@@ -39,7 +42,7 @@ def tile_fast_tucker_taylor_pa_t_kernel(tc, z, G2, grad_out, out):
         turned_go = ctx.enter_context(tc.tile_pool(name="turned_go", bufs=2 * ROUND))
         vector_kron = ctx.enter_context(tc.tile_pool(name="vector_kron", bufs=2))
         gpsimd_kron = ctx.enter_context(tc.tile_pool(name="gpsimd_kron", bufs=1))
-        scalar_kron = ctx.enter_context(tc.tile_pool(name="scalar_kron", bufs=2))
+        shared_kron = ctx.enter_context(tc.tile_pool(name="shared_kron", bufs=2))
         quantised = ctx.enter_context(tc.tile_pool(name="quantised", bufs=ROUND + 2))
         results = ctx.enter_context(tc.tile_pool(name="results", bufs=Q_TILES))
         psum_sums = ctx.enter_context(tc.psum_pool(name="psum_sums", bufs=1))
@@ -47,10 +50,13 @@ def tile_fast_tucker_taylor_pa_t_kernel(tc, z, G2, grad_out, out):
         psum_turn = ctx.enter_context(tc.psum_pool(name="psum_turn", bufs=3))
         ctx.enter_context(tc.manual_schedule())
 
-        n_slabs = 3 * RANK * SAMPLES // (PAIR * P * P)
-        z_runs = z.rearrange("j r (s w) -> (j r s) w", w=PAIR * P)
-        z_raw = keep.tile([P, n_slabs, PAIR * P], BF16)
-        nc.sync.dma_start(out=z_raw[:], in_=z_runs.rearrange("(m i) w -> i m w", i=P))
+        n_slabs = RANK * SAMPLES // (PAIR * P * P)
+        z_runs = z.rearrange("j r (s w) -> j (r s) w", w=PAIR * P)
+        z_raw = []
+        for j in range(3):
+            z_slabs = keep.tile([P, n_slabs, PAIR * P], BF16, name="z_slabs%d" % j)
+            nc.sync.dma_start(out=z_slabs[:], in_=z_runs[j].rearrange("(m i) w -> i m w", i=P))
+            z_raw.append(z_slabs)
 
         chunk_samples = CHUNK_PASSES * PASS
         go_rows = grad_out.rearrange("(qt i) n -> i qt n", i=P)
@@ -65,16 +71,13 @@ def tile_fast_tucker_taylor_pa_t_kernel(tc, z, G2, grad_out, out):
         identity = keep.tile([P, P], F32)
         make_identity(nc, identity[:])
 
-        slabs_per_factor = n_slabs // 3
         z_banks = []
         for j in range(3):
             pool = psum_z2 if j == 2 else psum_turn
             z_bank = pool.tile([P, BANK], F32, tag="z2" if j == 2 else "turned", name="z_bank%d" % j)
-            for i in range(slabs_per_factor):
+            for m in range(n_slabs):
                 nc.tensor.transpose(
-                    z_bank[:, i * P : (i + 1) * P],
-                    z_raw[:, j * slabs_per_factor + i, :].bitcast(F32),
-                    identity[:],
+                    z_bank[:, m * P : (m + 1) * P], z_raw[j][:, m, :].bitcast(F32), identity[:]
                 )
             z_banks.append(z_bank)
 
@@ -90,12 +93,17 @@ def tile_fast_tucker_taylor_pa_t_kernel(tc, z, G2, grad_out, out):
         z2_f32 = keep.tile([P, RANK, N_PASSES, PACK], F32)
         nc.scalar.copy(out=z2_f32[:], in_=z2_psum)
 
+        z1_psum = z_banks[1][:].bitcast(BF16).rearrange("p (b g t) -> p g b t", b=RANK, t=PACK)
         z01 = keep.tile([P, N_PASSES, RANK2, PACK], F32)
         for b in range(RANK):
-            nc.vector.tensor_tensor(
+            if b < RANK - GPSIMD_ROWS:
+                engine, z1_rows = nc.vector, z1_psum
+            else:
+                engine, z1_rows = nc.gpsimd, z_by_pass[1]
+            engine.tensor_tensor(
                 out=z01[:, :, b * RANK : (b + 1) * RANK, :],
                 in0=z_by_pass[0][:],
-                in1=z_by_pass[1][:, :, b : b + 1, :].to_broadcast([P, N_PASSES, RANK, PACK]),
+                in1=z1_rows[:, :, b : b + 1, :].to_broadcast([P, N_PASSES, RANK, PACK]),
                 op=MULT,
             )
 
@@ -126,76 +134,65 @@ def tile_fast_tucker_taylor_pa_t_kernel(tc, z, G2, grad_out, out):
                 )
             return grouped
 
-        def kron_as_tensors(engine, pool, z2_rows, g, cs):
-            part = pool.tile([P, len(cs) * RANK2 * PACK], BF16, align_bytes=64, tag="c%d" % len(cs))
-            shape = [P, len(cs), RANK2, PACK]
+        def multiply_tensors(engine, z2_rows, kron_bf, g, first_c, n_c):
+            cs = slice(first_c, first_c + n_c)
+            shape = [P, n_c, RANK2, PACK]
             engine.tensor_tensor(
-                out=part[:].rearrange("p (c x t) -> p c x t", x=RANK2, t=PACK),
+                out=kron_bf[:].rearrange("p (c x t) -> p c x t", x=RANK2, t=PACK)[:, cs, :, :],
                 in0=z01[:, g : g + 1, :, :].to_broadcast(shape),
-                in1=z2_rows[:, cs[0] : cs[0] + len(cs), g : g + 1, :].to_broadcast(shape),
+                in1=z2_rows[:, cs, g : g + 1, :].to_broadcast(shape),
                 op=MULT,
             )
-            return part
 
-        def kron_on_vector(g, cs):
-            return kron_as_tensors(nc.vector, vector_kron, z2_psum, g, cs)
-
-        def kron_on_gpsimd(g, cs):
-            return kron_as_tensors(nc.gpsimd, gpsimd_kron, z2_f32, g, cs)
-
-        def kron_on_scalar(g, cs):
-            part = scalar_kron.tile([P, len(cs) * RANK2 * PACK], BF16, align_bytes=64)
-            part_rows = part[:].rearrange("p (c x t) -> p c x t", x=RANK2, t=PACK)
-            for i in range(len(cs)):
+        def scale_on_scalar(kron_bf, g, first_c, n_c):
+            kron_rows = kron_bf[:].rearrange("p (c x t) -> p c x t", x=RANK2, t=PACK)
+            for c in range(first_c, first_c + n_c):
                 for t in range(PACK):
                     nc.scalar.activation(
-                        out=part_rows[:, i, :, t],
+                        out=kron_rows[:, c, :, t],
                         in_=z01[:, g, :, t],
                         func=COPY,
-                        scale=z2_f32[:, cs[i], g, t : t + 1],
+                        scale=z2_f32[:, c, g, t : t + 1],
                     )
-            return part
 
-        def quantise(parts, x4_dtype, operand):
+        def start_shared_pass(g):
+            kron_bf = shared_kron.tile([P, K * PACK], BF16, align_bytes=64)
+            scale_on_scalar(kron_bf, g, RANK - SCALAR_ROWS, SCALAR_ROWS)
+            return kron_bf
+
+        def quantise(values, x4_dtype, operand):
             codes_name, scales_name = "%s_codes" % operand, "%s_scales" % operand
             codes = quantised.tile([P, BANK], U32, align_bytes=64, name=codes_name, tag=codes_name)
             scales = quantised.tile([P, BANK], U8, align_bytes=64, name=scales_name, tag=scales_name)
-            first_row = 0
-            for part in parts:
-                n_rows = part.shape[1] // PACK
-                rows = slice(first_row, first_row + n_rows)
-                nc.vector.quantize_mx(
-                    out=codes[:, rows].bitcast(x4_dtype), scales=scales[:, rows], in_=part[:]
-                )
-                first_row += n_rows
+            nc.vector.quantize_mx(out=codes[:].bitcast(x4_dtype), scales=scales[:], in_=values[:])
             return codes, scales
 
-        all_c = range(RANK)
-        low_c = range(RANK // 2)
-        high_c = range(RANK // 2, RANK)
-        shared = ROUND - 2
         n_rounds = N_PASSES // ROUND
-
         go_next = [turn_grad_out(g) for g in range(ROUND)]
-        scalar_next = kron_on_scalar(shared, high_c)
+        shared_next = start_shared_pass(SHARED)
 
         for r in range(n_rounds):
             first = r * ROUND
-            go_now, scalar_now = go_next, scalar_next
-            kron_now = [
-                [kron_on_vector(first, all_c)],
-                [kron_on_vector(first + 1, all_c)],
-                [kron_on_vector(first + shared, low_c), scalar_now],
-                [kron_on_gpsimd(first + ROUND - 1, all_c)],
-            ]
+            go_now, shared_now = go_next, shared_next
+
+            kron_now = []
+            for g in range(first, first + SHARED):
+                kron_bf = vector_kron.tile([P, K * PACK], BF16, align_bytes=64)
+                multiply_tensors(nc.vector, z2_psum, kron_bf, g, 0, RANK)
+                kron_now.append(kron_bf)
+            multiply_tensors(nc.vector, z2_psum, shared_now, first + SHARED, 0, RANK - SCALAR_ROWS)
+            kron_now.append(shared_now)
+            kron_bf = gpsimd_kron.tile([P, K * PACK], BF16, align_bytes=64)
+            multiply_tensors(nc.gpsimd, z2_f32, kron_bf, first + ROUND - 1, 0, RANK)
+            kron_now.append(kron_bf)
 
             if r + 1 < n_rounds:
                 go_next = [turn_grad_out(first + ROUND + i) for i in range(ROUND)]
-                scalar_next = kron_on_scalar(first + ROUND + shared, high_c)
+                shared_next = start_shared_pass(first + ROUND + SHARED)
 
             for i in range(ROUND):
                 g = first + i
-                go_codes, go_scales = quantise([go_now[i]], E5M2_X4, "go")
+                go_codes, go_scales = quantise(go_now[i], E5M2_X4, "go")
                 kron_codes, kron_scales = quantise(kron_now[i], E4M3_X4, "kron")
 
                 for qt in range(Q_TILES):

@@ -43,6 +43,7 @@ def tile_fast_tucker_taylor_pa_t_kernel(tc, z, G2, grad_out, out):
         vector_kron = ctx.enter_context(tc.tile_pool(name="vector_kron", bufs=2))
         gpsimd_kron = ctx.enter_context(tc.tile_pool(name="gpsimd_kron", bufs=1))
         shared_kron = ctx.enter_context(tc.tile_pool(name="shared_kron", bufs=2))
+        staging = ctx.enter_context(tc.tile_pool(name="staging", bufs=2))
         quantised = ctx.enter_context(tc.tile_pool(name="quantised", bufs=ROUND + 2))
         results = ctx.enter_context(tc.tile_pool(name="results", bufs=Q_TILES))
         psum_sums = ctx.enter_context(tc.psum_pool(name="psum_sums", bufs=1))
@@ -145,15 +146,26 @@ def tile_fast_tucker_taylor_pa_t_kernel(tc, z, G2, grad_out, out):
             )
 
         def scale_on_scalar(kron_bf, g, first_c, n_c):
-            kron_rows = kron_bf[:].rearrange("p (c x t) -> p c x t", x=RANK2, t=PACK)
+            n_k = n_c * RANK2
+            kron_words = kron_bf[:].bitcast(F32).rearrange("p (k u) -> p k u", u=PAIR)
+            staged = staging.tile([P, PAIR, n_k, PAIR], BF16)
             for c in range(first_c, first_c + n_c):
                 for t in range(PACK):
                     nc.scalar.activation(
-                        out=kron_rows[:, c, :, t],
+                        out=staged[
+                            :, t // PAIR, (c - first_c) * RANK2 : (c - first_c + 1) * RANK2, t % PAIR
+                        ],
                         in_=z01[:, g, :, t],
                         func=COPY,
                         scale=z2_f32[:, c, g, t : t + 1],
                     )
+            nc.scalar.copy(
+                out=kron_words[:, first_c * RANK2 : (first_c + n_c) * RANK2, :],
+                in_=staged[:]
+                .rearrange("p u k e -> p (u k e)")
+                .bitcast(F32)
+                .rearrange("p (u k) -> p k u", u=PAIR),
+            )
 
         def start_shared_pass(g):
             kron_bf = shared_kron.tile([P, K * PACK], BF16, align_bytes=64)

@@ -29,6 +29,9 @@ ROUND = 4
 SHARED = ROUND - 2
 SCALAR_ROWS = 6
 GPSIMD_ROWS = 2
+LATE_FROM_VECTOR = 3
+LATE_FROM_GPSIMD = 2
+KEEP_WARM = 12
 
 FLOPS = 2 * Q * K * SAMPLES
 BYTES = 3 * RANK * SAMPLES * 2 + Q * SAMPLES * 2 + Q * K * 4
@@ -52,12 +55,19 @@ def tile_fast_tucker_taylor_pa_t_kernel(tc, z, G2, grad_out, out):
         ctx.enter_context(tc.manual_schedule())
 
         n_slabs = RANK * SAMPLES // (PAIR * P * P)
+        slab_rows = RANK // n_slabs
         z_runs = z.rearrange("j r (s w) -> j (r s) w", w=PAIR * P)
-        z_raw = []
-        for j in range(3):
-            z_slabs = keep.tile([P, n_slabs, PAIR * P], BF16, name="z_slabs%d" % j)
-            nc.sync.dma_start(out=z_slabs[:], in_=z_runs[j].rearrange("(m i) w -> i m w", i=P))
-            z_raw.append(z_slabs)
+        z_raw = [
+            [keep.tile([P, PAIR * P], BF16, name="z%d_slab%d" % (j, m)) for m in range(n_slabs)]
+            for j in range(3)
+        ]
+        z1_order = [0, 3, 2, 1]
+        for j, m in (
+            [(0, m) for m in range(n_slabs)]
+            + [(1, m) for m in z1_order]
+            + [(2, m) for m in range(n_slabs)]
+        ):
+            nc.sync.dma_start(out=z_raw[j][m][:], in_=z_runs[j][m * P : (m + 1) * P, :])
 
         chunk_samples = CHUNK_PASSES * PASS
         go_rows = grad_out.rearrange("(qt i) n -> i qt n", i=P)
@@ -69,46 +79,78 @@ def tile_fast_tucker_taylor_pa_t_kernel(tc, z, G2, grad_out, out):
             )
             go_chunks.append(go_sb)
 
+        zeros = keep.tile([P, BANK], BF16)
+        nc.vector.memset(zeros[:], 0.0)
         identity = keep.tile([P, P], F32)
         make_identity(nc, identity[:])
 
-        z_banks = []
-        for j in range(3):
-            pool = psum_z2 if j == 2 else psum_turn
-            z_bank = pool.tile([P, BANK], F32, tag="z2" if j == 2 else "turned", name="z_bank%d" % j)
-            for m in range(n_slabs):
-                nc.tensor.transpose(
-                    z_bank[:, m * P : (m + 1) * P], z_raw[j][:, m, :].bitcast(F32), identity[:]
-                )
-            z_banks.append(z_bank)
+        def turn_slab(out_columns, j, m):
+            nc.tensor.transpose(out_columns, z_raw[j][m][:].bitcast(F32), identity[:])
 
-        z_by_pass = []
-        for j in range(2):
-            z_sb = keep.tile([P, N_PASSES, RANK, PACK], BF16, name="z_sb%d" % j)
-            nc.scalar.copy(
-                out=z_sb[:].bitcast(F32),
-                in_=z_banks[j][:].rearrange("p (r g u) -> p g r u", r=RANK, u=PAIR),
-            )
-            z_by_pass.append(z_sb)
-        z2_psum = z_banks[2][:].bitcast(BF16).rearrange("p (c g t) -> p c g t", c=RANK, t=PACK)
+        z0_bank = psum_turn.tile([P, BANK], F32, tag="turned")
+        for m in range(n_slabs):
+            turn_slab(z0_bank[:, m * P : (m + 1) * P], 0, m)
+        z1_turned = [
+            psum_sums.tile([P, P], F32, name="z1_turned%d" % m, tag="sums%d" % m)
+            for m in range(n_slabs)
+        ]
+        for m in z1_order:
+            turn_slab(z1_turned[m][:], 1, m)
+        z2_bank = psum_z2.tile([P, BANK], F32)
+        for m in range(n_slabs):
+            turn_slab(z2_bank[:, m * P : (m + 1) * P], 2, m)
+
+        z0_sb = keep.tile([P, N_PASSES, RANK, PACK], BF16)
+        nc.vector.tensor_copy(
+            out=z0_sb[:].bitcast(F32),
+            in_=z0_bank[:].rearrange("p (r g u) -> p g r u", r=RANK, u=PAIR),
+        )
+        split_row = RANK - GPSIMD_ROWS - 1
+        z1_sb = keep.tile([P, N_PASSES, RANK, PACK], BF16)
+        for m in z1_order:
+            if (m + 1) * slab_rows > split_row:
+                nc.scalar.copy(
+                    out=z1_sb[:].bitcast(F32)[:, :, m * slab_rows : (m + 1) * slab_rows, :],
+                    in_=z1_turned[m][:].rearrange("p (r g u) -> p g r u", r=slab_rows, u=PAIR),
+                )
+        z2_psum = z2_bank[:].bitcast(BF16).rearrange("p (c g t) -> p c g t", c=RANK, t=PACK)
         z2_f32 = keep.tile([P, RANK, N_PASSES, PACK], F32)
         nc.scalar.copy(out=z2_f32[:], in_=z2_psum)
 
-        z1_psum = z_banks[1][:].bitcast(BF16).rearrange("p (b g t) -> p g b t", b=RANK, t=PACK)
         z01 = keep.tile([P, N_PASSES, RANK2, PACK], F32)
-        for b in range(RANK):
-            if b < RANK - GPSIMD_ROWS:
-                engine, z1_rows = nc.vector, z1_psum
+
+        def multiply_z0_z1(on_vector, b, first_g, n_g):
+            gs = slice(first_g, first_g + n_g)
+            if on_vector:
+                engine = nc.vector
+                z1_row = (
+                    z1_turned[b // slab_rows][:]
+                    .bitcast(BF16)
+                    .rearrange("p (r g t) -> p g r t", r=slab_rows, t=PACK)[
+                        :, gs, b % slab_rows : b % slab_rows + 1, :
+                    ]
+                )
             else:
-                engine, z1_rows = nc.gpsimd, z_by_pass[1]
+                engine = nc.gpsimd
+                z1_row = z1_sb[:, gs, b : b + 1, :]
             engine.tensor_tensor(
-                out=z01[:, :, b * RANK : (b + 1) * RANK, :],
-                in0=z_by_pass[0][:],
-                in1=z1_rows[:, :, b : b + 1, :].to_broadcast([P, N_PASSES, RANK, PACK]),
+                out=z01[:, gs, b * RANK : (b + 1) * RANK, :],
+                in0=z0_sb[:, gs, :, :],
+                in1=z1_row.to_broadcast([P, n_g, RANK, PACK]),
                 op=MULT,
             )
 
-        sums = [psum_sums.tile([P, K], F32, name="sums%d" % qt) for qt in range(Q_TILES)]
+        for b in range(split_row):
+            multiply_z0_z1(True, b, 0, N_PASSES)
+        multiply_z0_z1(True, split_row, 0, N_PASSES // 2)
+        for b in range(split_row + 1, RANK):
+            multiply_z0_z1(False, b, 0, N_PASSES)
+        multiply_z0_z1(False, split_row, N_PASSES // 2, N_PASSES // 2)
+
+        sums = [
+            psum_sums.tile([P, K], F32, name="sums%d" % qt, tag="sums%d" % qt)
+            for qt in range(Q_TILES)
+        ]
 
         def turn_grad_out(g):
             go_words = go_chunks[g // CHUNK_PASSES][:].bitcast(F32)
@@ -186,19 +228,33 @@ def tile_fast_tucker_taylor_pa_t_kernel(tc, z, G2, grad_out, out):
         for r in range(n_rounds):
             first = r * ROUND
             go_now, shared_now = go_next, shared_next
+            last_round = r + 1 == n_rounds
+            vector_rows = [RANK, RANK - LATE_FROM_VECTOR if last_round else RANK]
+            shared_rows = 0 if last_round else RANK - SCALAR_ROWS
+            gpsimd_rows = RANK - LATE_FROM_GPSIMD if last_round else RANK
 
             kron_now = []
-            for g in range(first, first + SHARED):
+            for i in range(SHARED):
                 kron_bf = vector_kron.tile([P, K * PACK], BF16, align_bytes=64)
-                multiply_tensors(nc.vector, z2_psum, kron_bf, g, 0, RANK)
+                multiply_tensors(nc.vector, z2_psum, kron_bf, first + i, 0, vector_rows[i])
                 kron_now.append(kron_bf)
-            multiply_tensors(nc.vector, z2_psum, shared_now, first + SHARED, 0, RANK - SCALAR_ROWS)
+            if shared_rows > 0:
+                multiply_tensors(nc.vector, z2_psum, shared_now, first + SHARED, 0, shared_rows)
             kron_now.append(shared_now)
             kron_bf = gpsimd_kron.tile([P, K * PACK], BF16, align_bytes=64)
-            multiply_tensors(nc.gpsimd, z2_f32, kron_bf, first + ROUND - 1, 0, RANK)
+            multiply_tensors(nc.gpsimd, z2_f32, kron_bf, first + ROUND - 1, 0, gpsimd_rows)
             kron_now.append(kron_bf)
 
-            if r + 1 < n_rounds:
+            if last_round:
+                scale_on_scalar(kron_now[1], first + 1, vector_rows[1], RANK - vector_rows[1])
+                scale_on_scalar(shared_now, first + SHARED, 0, RANK - SCALAR_ROWS)
+                scale_on_scalar(kron_bf, first + ROUND - 1, gpsimd_rows, RANK - gpsimd_rows)
+                unused = psum_turn.tile([P, BANK], F32, tag="turned")
+                for i in range(KEEP_WARM):
+                    nc.tensor.matmul(
+                        unused[:], lhsT=zeros[:, :P], rhs=zeros[:], start=True, stop=True
+                    )
+            else:
                 go_next = [turn_grad_out(first + ROUND + i) for i in range(ROUND)]
                 shared_next = start_shared_pass(first + ROUND + SHARED)
 

@@ -29,9 +29,7 @@ ROUND = 4
 SHARED = ROUND - 2
 SCALAR_ROWS = 6
 GPSIMD_ROWS = 2
-LATE_FROM_VECTOR = 3
-LATE_FROM_GPSIMD = 2
-KEEP_WARM = 12
+KEEP_WARM = 16
 
 FLOPS = 2 * Q * K * SAMPLES
 BYTES = 3 * RANK * SAMPLES * 2 + Q * SAMPLES * 2 + Q * K * 4
@@ -228,35 +226,27 @@ def tile_fast_tucker_taylor_pa_t_kernel(tc, z, G2, grad_out, out):
         for r in range(n_rounds):
             first = r * ROUND
             go_now, shared_now = go_next, shared_next
-            last_round = r + 1 == n_rounds
-            vector_rows = [RANK, RANK - LATE_FROM_VECTOR if last_round else RANK]
-            shared_rows = 0 if last_round else RANK - SCALAR_ROWS
-            gpsimd_rows = RANK - LATE_FROM_GPSIMD if last_round else RANK
 
             kron_now = []
-            for i in range(SHARED):
+            for g in range(first, first + SHARED):
                 kron_bf = vector_kron.tile([P, K * PACK], BF16, align_bytes=64)
-                multiply_tensors(nc.vector, z2_psum, kron_bf, first + i, 0, vector_rows[i])
+                multiply_tensors(nc.vector, z2_psum, kron_bf, g, 0, RANK)
                 kron_now.append(kron_bf)
-            if shared_rows > 0:
-                multiply_tensors(nc.vector, z2_psum, shared_now, first + SHARED, 0, shared_rows)
+            multiply_tensors(nc.vector, z2_psum, shared_now, first + SHARED, 0, RANK - SCALAR_ROWS)
             kron_now.append(shared_now)
             kron_bf = gpsimd_kron.tile([P, K * PACK], BF16, align_bytes=64)
-            multiply_tensors(nc.gpsimd, z2_f32, kron_bf, first + ROUND - 1, 0, gpsimd_rows)
+            multiply_tensors(nc.gpsimd, z2_f32, kron_bf, first + ROUND - 1, 0, RANK)
             kron_now.append(kron_bf)
 
-            if last_round:
-                scale_on_scalar(kron_now[1], first + 1, vector_rows[1], RANK - vector_rows[1])
-                scale_on_scalar(shared_now, first + SHARED, 0, RANK - SCALAR_ROWS)
-                scale_on_scalar(kron_bf, first + ROUND - 1, gpsimd_rows, RANK - gpsimd_rows)
+            if r + 1 < n_rounds:
+                go_next = [turn_grad_out(first + ROUND + i) for i in range(ROUND)]
+                shared_next = start_shared_pass(first + ROUND + SHARED)
+            else:
                 unused = psum_turn.tile([P, BANK], F32, tag="turned")
                 for i in range(KEEP_WARM):
                     nc.tensor.matmul(
                         unused[:], lhsT=zeros[:, :P], rhs=zeros[:], start=True, stop=True
                     )
-            else:
-                go_next = [turn_grad_out(first + ROUND + i) for i in range(ROUND)]
-                shared_next = start_shared_pass(first + ROUND + SHARED)
 
             for i in range(ROUND):
                 g = first + i

@@ -29,7 +29,6 @@ ROUND = 4
 SHARED = ROUND - 2
 SCALAR_ROWS = 6
 GPSIMD_ROWS = 2
-KEEP_WARM = 16
 
 FLOPS = 2 * Q * K * SAMPLES
 BYTES = 3 * RANK * SAMPLES * 2 + Q * SAMPLES * 2 + Q * K * 4
@@ -77,8 +76,6 @@ def tile_fast_tucker_taylor_pa_t_kernel(tc, z, G2, grad_out, out):
             )
             go_chunks.append(go_sb)
 
-        zeros = keep.tile([P, BANK], BF16)
-        nc.vector.memset(zeros[:], 0.0)
         identity = keep.tile([P, P], F32)
         make_identity(nc, identity[:])
 
@@ -103,10 +100,10 @@ def tile_fast_tucker_taylor_pa_t_kernel(tc, z, G2, grad_out, out):
             out=z0_sb[:].bitcast(F32),
             in_=z0_bank[:].rearrange("p (r g u) -> p g r u", r=RANK, u=PAIR),
         )
-        split_row = RANK - GPSIMD_ROWS - 1
+        first_gpsimd_row = RANK - GPSIMD_ROWS
         z1_sb = keep.tile([P, N_PASSES, RANK, PACK], BF16)
         for m in z1_order:
-            if (m + 1) * slab_rows > split_row:
+            if (m + 1) * slab_rows > first_gpsimd_row:
                 nc.scalar.copy(
                     out=z1_sb[:].bitcast(F32)[:, :, m * slab_rows : (m + 1) * slab_rows, :],
                     in_=z1_turned[m][:].rearrange("p (r g u) -> p g r u", r=slab_rows, u=PAIR),
@@ -138,12 +135,8 @@ def tile_fast_tucker_taylor_pa_t_kernel(tc, z, G2, grad_out, out):
                 op=MULT,
             )
 
-        for b in range(split_row):
-            multiply_z0_z1(True, b, 0, N_PASSES)
-        multiply_z0_z1(True, split_row, 0, N_PASSES // 2)
-        for b in range(split_row + 1, RANK):
-            multiply_z0_z1(False, b, 0, N_PASSES)
-        multiply_z0_z1(False, split_row, N_PASSES // 2, N_PASSES // 2)
+        for b in range(RANK):
+            multiply_z0_z1(b < first_gpsimd_row, b, 0, N_PASSES)
 
         sums = [
             psum_sums.tile([P, K], F32, name="sums%d" % qt, tag="sums%d" % qt)
@@ -241,12 +234,6 @@ def tile_fast_tucker_taylor_pa_t_kernel(tc, z, G2, grad_out, out):
             if r + 1 < n_rounds:
                 go_next = [turn_grad_out(first + ROUND + i) for i in range(ROUND)]
                 shared_next = start_shared_pass(first + ROUND + SHARED)
-            else:
-                unused = psum_turn.tile([P, BANK], F32, tag="turned")
-                for i in range(KEEP_WARM):
-                    nc.tensor.matmul(
-                        unused[:], lhsT=zeros[:, :P], rhs=zeros[:], start=True, stop=True
-                    )
 
             for i in range(ROUND):
                 g = first + i

@@ -28,7 +28,7 @@ CHUNK_PASSES = 2
 ROUND = 4
 SHARED = ROUND - 2
 SCALAR_ROWS = 6
-GPSIMD_ROWS = 2
+GPSIMD_ROWS = 1
 
 FLOPS = 2 * Q * K * SAMPLES
 BYTES = 3 * RANK * SAMPLES * 2 + Q * SAMPLES * 2 + Q * K * 4

from contextlib import ExitStack

import concourse.mybir as mybir
from concourse.masks import make_identity

F32 = mybir.dt.float32
BF16 = mybir.dt.bfloat16
U32 = mybir.dt.uint32
U8 = mybir.dt.uint8
E4M3_X4 = mybir.dt.float8_e4m3fn_x4
E5M2_X4 = mybir.dt.float8_e5m2_x4
MULT = mybir.AluOpType.mult
COPY = mybir.ActivationFunctionType.Copy

P = 128
PACK = 4
PAIR = 2
PASS = P * PACK
RANK = 8
RANK2 = RANK * RANK
Q = 512
K = RANK * RANK2
SAMPLES = 16384
N_PASSES = SAMPLES // PASS
Q_TILES = Q // P
BANK = 512
CHUNK_PASSES = 2
ROUND = 4
SHARED = ROUND - 2
SCALAR_ROWS = 6
GPSIMD_ROWS = 1

FLOPS = 2 * Q * K * SAMPLES
BYTES = 3 * RANK * SAMPLES * 2 + Q * SAMPLES * 2 + Q * K * 4


def tile_fast_tucker_taylor_pa_t_kernel(tc, z, G2, grad_out, out):
    nc = tc.nc
    with ExitStack() as ctx:
        keep = ctx.enter_context(tc.tile_pool(name="keep", bufs=1))
        loads = ctx.enter_context(tc.tile_pool(name="loads", bufs=6))
        turned_go = ctx.enter_context(tc.tile_pool(name="turned_go", bufs=2 * ROUND))
        vector_kron = ctx.enter_context(tc.tile_pool(name="vector_kron", bufs=2))
        gpsimd_kron = ctx.enter_context(tc.tile_pool(name="gpsimd_kron", bufs=1))
        shared_kron = ctx.enter_context(tc.tile_pool(name="shared_kron", bufs=2))
        staging = ctx.enter_context(tc.tile_pool(name="staging", bufs=2))
        quantised = ctx.enter_context(tc.tile_pool(name="quantised", bufs=ROUND + 2))
        results = ctx.enter_context(tc.tile_pool(name="results", bufs=Q_TILES))
        psum_sums = ctx.enter_context(tc.psum_pool(name="psum_sums", bufs=1))
        psum_z2 = ctx.enter_context(tc.psum_pool(name="psum_z2", bufs=1))
        psum_turn = ctx.enter_context(tc.psum_pool(name="psum_turn", bufs=3))
        ctx.enter_context(tc.manual_schedule())

        n_slabs = RANK * SAMPLES // (PAIR * P * P)
        slab_rows = RANK // n_slabs
        z_runs = z.rearrange("j r (s w) -> j (r s) w", w=PAIR * P)
        z_raw = [
            [keep.tile([P, PAIR * P], BF16, name="z%d_slab%d" % (j, m)) for m in range(n_slabs)]
            for j in range(3)
        ]
        z1_order = [0, 3, 2, 1]
        for j, m in (
            [(0, m) for m in range(n_slabs)]
            + [(1, m) for m in z1_order]
            + [(2, m) for m in range(n_slabs)]
        ):
            nc.sync.dma_start(out=z_raw[j][m][:], in_=z_runs[j][m * P : (m + 1) * P, :])

        chunk_samples = CHUNK_PASSES * PASS
        go_rows = grad_out.rearrange("(qt i) n -> i qt n", i=P)
        go_chunks = []
        for c in range(N_PASSES // CHUNK_PASSES):
            go_sb = loads.tile([P, Q_TILES, chunk_samples], BF16)
            nc.sync.dma_start(
                out=go_sb[:], in_=go_rows[:, :, c * chunk_samples : (c + 1) * chunk_samples]
            )
            go_chunks.append(go_sb)

        identity = keep.tile([P, P], F32)
        make_identity(nc, identity[:])

        def turn_slab(out_columns, j, m):
            nc.tensor.transpose(out_columns, z_raw[j][m][:].bitcast(F32), identity[:])

        z0_bank = psum_turn.tile([P, BANK], F32, tag="turned")
        for m in range(n_slabs):
            turn_slab(z0_bank[:, m * P : (m + 1) * P], 0, m)
        z1_turned = [
            psum_sums.tile([P, P], F32, name="z1_turned%d" % m, tag="sums%d" % m)
            for m in range(n_slabs)
        ]
        for m in z1_order:
            turn_slab(z1_turned[m][:], 1, m)
        z2_bank = psum_z2.tile([P, BANK], F32)
        for m in range(n_slabs):
            turn_slab(z2_bank[:, m * P : (m + 1) * P], 2, m)

        z0_sb = keep.tile([P, N_PASSES, RANK, PACK], BF16)
        nc.vector.tensor_copy(
            out=z0_sb[:].bitcast(F32),
            in_=z0_bank[:].rearrange("p (r g u) -> p g r u", r=RANK, u=PAIR),
        )
        first_gpsimd_row = RANK - GPSIMD_ROWS
        z1_sb = keep.tile([P, N_PASSES, RANK, PACK], BF16)
        for m in z1_order:
            if (m + 1) * slab_rows > first_gpsimd_row:
                nc.scalar.copy(
                    out=z1_sb[:].bitcast(F32)[:, :, m * slab_rows : (m + 1) * slab_rows, :],
                    in_=z1_turned[m][:].rearrange("p (r g u) -> p g r u", r=slab_rows, u=PAIR),
                )
        z2_psum = z2_bank[:].bitcast(BF16).rearrange("p (c g t) -> p c g t", c=RANK, t=PACK)
        z2_f32 = keep.tile([P, RANK, N_PASSES, PACK], F32)
        nc.scalar.copy(out=z2_f32[:], in_=z2_psum)

        z01 = keep.tile([P, N_PASSES, RANK2, PACK], F32)

        def multiply_z0_z1(on_vector, b, first_g, n_g):
            gs = slice(first_g, first_g + n_g)
            if on_vector:
                engine = nc.vector
                z1_row = (
                    z1_turned[b // slab_rows][:]
                    .bitcast(BF16)
                    .rearrange("p (r g t) -> p g r t", r=slab_rows, t=PACK)[
                        :, gs, b % slab_rows : b % slab_rows + 1, :
                    ]
                )
            else:
                engine = nc.gpsimd
                z1_row = z1_sb[:, gs, b : b + 1, :]
            engine.tensor_tensor(
                out=z01[:, gs, b * RANK : (b + 1) * RANK, :],
                in0=z0_sb[:, gs, :, :],
                in1=z1_row.to_broadcast([P, n_g, RANK, PACK]),
                op=MULT,
            )

        for b in range(RANK):
            multiply_z0_z1(b < first_gpsimd_row, b, 0, N_PASSES)

        sums = [
            psum_sums.tile([P, K], F32, name="sums%d" % qt, tag="sums%d" % qt)
            for qt in range(Q_TILES)
        ]

        def turn_grad_out(g):
            go_words = go_chunks[g // CHUNK_PASSES][:].bitcast(F32)
            first_word = (g % CHUNK_PASSES) * PASS // PAIR
            grouped = turned_go.tile([P, Q * PACK], BF16, align_bytes=64)
            grouped_words = grouped[:].bitcast(F32).rearrange("p (q u) -> p q u", u=PAIR)
            rows_per_bank = BANK // PAIR
            for h in range(Q // rows_per_bank):
                turned = psum_turn.tile([P, PAIR, rows_per_bank], F32, tag="turned")
                for u in range(PAIR):
                    for i in range(rows_per_bank // P):
                        nc.tensor.transpose(
                            turned[:, u, i * P : (i + 1) * P],
                            go_words[
                                :,
                                h * (rows_per_bank // P) + i,
                                first_word + u * P : first_word + (u + 1) * P,
                            ],
                            identity[:],
                        )
                nc.scalar.copy(
                    out=grouped_words[:, h * rows_per_bank : (h + 1) * rows_per_bank, :],
                    in_=turned[:].rearrange("p u q -> p q u"),
                )
            return grouped

        def multiply_tensors(engine, z2_rows, kron_bf, g, first_c, n_c):
            cs = slice(first_c, first_c + n_c)
            shape = [P, n_c, RANK2, PACK]
            engine.tensor_tensor(
                out=kron_bf[:].rearrange("p (c x t) -> p c x t", x=RANK2, t=PACK)[:, cs, :, :],
                in0=z01[:, g : g + 1, :, :].to_broadcast(shape),
                in1=z2_rows[:, cs, g : g + 1, :].to_broadcast(shape),
                op=MULT,
            )

        def scale_on_scalar(kron_bf, g, first_c, n_c):
            n_k = n_c * RANK2
            kron_words = kron_bf[:].bitcast(F32).rearrange("p (k u) -> p k u", u=PAIR)
            staged = staging.tile([P, PAIR, n_k, PAIR], BF16)
            for c in range(first_c, first_c + n_c):
                for t in range(PACK):
                    nc.scalar.activation(
                        out=staged[
                            :, t // PAIR, (c - first_c) * RANK2 : (c - first_c + 1) * RANK2, t % PAIR
                        ],
                        in_=z01[:, g, :, t],
                        func=COPY,
                        scale=z2_f32[:, c, g, t : t + 1],
                    )
            nc.scalar.copy(
                out=kron_words[:, first_c * RANK2 : (first_c + n_c) * RANK2, :],
                in_=staged[:]
                .rearrange("p u k e -> p (u k e)")
                .bitcast(F32)
                .rearrange("p (u k) -> p k u", u=PAIR),
            )

        def start_shared_pass(g):
            kron_bf = shared_kron.tile([P, K * PACK], BF16, align_bytes=64)
            scale_on_scalar(kron_bf, g, RANK - SCALAR_ROWS, SCALAR_ROWS)
            return kron_bf

        def quantise(values, x4_dtype, operand):
            codes_name, scales_name = "%s_codes" % operand, "%s_scales" % operand
            codes = quantised.tile([P, BANK], U32, align_bytes=64, name=codes_name, tag=codes_name)
            scales = quantised.tile([P, BANK], U8, align_bytes=64, name=scales_name, tag=scales_name)
            nc.vector.quantize_mx(out=codes[:].bitcast(x4_dtype), scales=scales[:], in_=values[:])
            return codes, scales

        n_rounds = N_PASSES // ROUND
        go_next = [turn_grad_out(g) for g in range(ROUND)]
        shared_next = start_shared_pass(SHARED)

        for r in range(n_rounds):
            first = r * ROUND
            go_now, shared_now = go_next, shared_next

            kron_now = []
            for g in range(first, first + SHARED):
                kron_bf = vector_kron.tile([P, K * PACK], BF16, align_bytes=64)
                multiply_tensors(nc.vector, z2_psum, kron_bf, g, 0, RANK)
                kron_now.append(kron_bf)
            multiply_tensors(nc.vector, z2_psum, shared_now, first + SHARED, 0, RANK - SCALAR_ROWS)
            kron_now.append(shared_now)
            kron_bf = gpsimd_kron.tile([P, K * PACK], BF16, align_bytes=64)
            multiply_tensors(nc.gpsimd, z2_f32, kron_bf, first + ROUND - 1, 0, RANK)
            kron_now.append(kron_bf)

            if r + 1 < n_rounds:
                go_next = [turn_grad_out(first + ROUND + i) for i in range(ROUND)]
                shared_next = start_shared_pass(first + ROUND + SHARED)

            for i in range(ROUND):
                g = first + i
                go_codes, go_scales = quantise(go_now[i], E5M2_X4, "go")
                kron_codes, kron_scales = quantise(kron_now[i], E4M3_X4, "kron")

                for qt in range(Q_TILES):
                    q_cols = slice(qt * P, (qt + 1) * P)
                    nc.tensor.matmul_mx(
                        out=sums[qt][:],
                        lhsT=go_codes[:, q_cols].bitcast(E5M2_X4),
                        lhsT_scale=go_scales[:, q_cols],
                        rhs=kron_codes[:].bitcast(E4M3_X4),
                        rhs_scale=kron_scales[:],
                        start=(g == 0),
                        stop=(g == N_PASSES - 1),
                    )

        for qt in range(Q_TILES):
            result = results.tile([P, K], F32)
            if qt % 2 == 0:
                nc.scalar.copy(out=result[:], in_=sums[qt][:])
            else:
                nc.vector.tensor_copy(out=result[:], in_=sums[qt][:])
            nc.sync.dma_start(out=out[qt * P : (qt + 1) * P, :], in_=result[:])
